import numpy as np
import ml_dtypes


def mxq(x, axis, fmt="e4m3"):
    dtype, down = {"e4m3": (ml_dtypes.float8_e4m3fn, 7), "e5m2": (ml_dtypes.float8_e5m2, 14)}[fmt]
    v = np.moveaxis(np.asarray(x, np.float32).astype(ml_dtypes.bfloat16).astype(np.float64), axis, -1)
    blocks = v.reshape(v.shape[:-1] + (-1, 32))
    amax = np.abs(blocks).max(-1, keepdims=True)
    byte = np.maximum(np.where(amax > 0, np.frexp(amax)[1] - 1 + 127, 0) - down, 1)
    scale = np.exp2(byte - 127.0)
    codes = (blocks / scale).astype(np.float32).astype(dtype).astype(np.float64)
    return np.moveaxis((codes * scale).reshape(v.shape), -1, axis)


WIDE = False


def mx_kscale(k):
    if not WIDE:
        return np.ones(k)
    levels = np.array([10, -10, 5, -5, 0])
    a = np.random.permutation(np.resize(levels, k // 512 * 4)).reshape(k // 512, 4)
    idx = np.arange(k)
    return np.exp2(a[idx // 512, idx % 128 // 32])


BF16 = ml_dtypes.bfloat16


def bf(x):
    return np.asarray(x, np.float32).astype(BF16)


def f64(x):
    return np.asarray(x).astype(np.float64)


B, C, P, Q, R = 8192, 512, 8, 8, 8
D = P * Q * R


def setup_inputs():
    s = mx_kscale(D).reshape(P, Q, R)
    return {"core": bf(np.random.standard_normal((B, P, Q, R)) * s),
            "weights": bf(np.random.standard_normal((C, P, Q, R)) / np.sqrt(D) / s)}


def reference(core, weights):
    b = core.shape[0]
    c = weights.shape[0]
    x = mxq(f64(core).reshape(b, -1), 1, "e4m3")
    w = mxq(f64(weights).reshape(c, -1), 1, "e4m3")
    return x @ w.T

@@ -1,0 +1,135 @@
+from contextlib import ExitStack
+
+import concourse.mybir as mybir
+from concourse.masks import make_identity
+
+F32 = mybir.dt.float32
+BF16 = mybir.dt.bfloat16
+U32 = mybir.dt.uint32
+U8 = mybir.dt.uint8
+FP8X4 = mybir.dt.float8_e4m3fn_x4
+
+P = 128
+B = 8192
+C = 512
+K = 512
+KW = K // 2
+T = B // P
+G = 4
+NG = T // G
+LOAD_TILES = [4, 4, 8, 16, 32]
+STORE_TILES = [8, 8, 8, 8, 8, 8, 8, 8]
+
+FLOPS = 2 * B * C * K
+
+
+def tile_tensoroutputlayer_t_kernel(tc, core, weights, out):
+    nc = tc.nc
+    core_v = core.rearrange("(p t) i j k -> p (t i j k)", t=T)
+    out_v = out.rearrange("(p t) c -> p (t c)", t=T)
+    w_v = weights.rearrange("(j p) a b c -> p j (a b c)", p=P)
+
+    with ExitStack() as ctx:
+        keep = ctx.enter_context(tc.tile_pool(name="keep", bufs=1))
+        stage = ctx.enter_context(tc.tile_pool(name="stage", bufs=3))
+        tps = ctx.enter_context(tc.psum_pool(name="tps", bufs=4))
+        ops = ctx.enter_context(tc.psum_pool(name="ops", bufs=4))
+        ctx.enter_context(tc.manual_schedule())
+
+        w_raw = keep.tile([P, G * K], BF16, name="w_raw")
+        nc.sync.dma_start(out=w_raw[:].rearrange("p (j k) -> p j k", j=G), in_=w_v)
+        x_of_tile = []
+        t0 = 0
+        for c, n in enumerate(LOAD_TILES):
+            x = keep.tile([P, n * K], BF16, name="x%d" % c)
+            nc.sync.dma_start(out=x[:], in_=core_v[:, t0 * K : (t0 + n) * K])
+            xw = x[:].bitcast(F32)
+            for i in range(n):
+                x_of_tile.append((xw, i))
+            t0 += n
+
+        ident = keep.tile([P, P], F32, name="ident")
+        make_identity(nc, ident[:])
+
+        o_of_tile = []
+        o_tiles = []
+        for c, n in enumerate(STORE_TILES):
+            o = keep.tile([P, n * C], F32, name="o%d" % c)
+            o_tiles.append(o)
+            for i in range(n):
+                o_of_tile.append((c, i, i == n - 1))
+
+        def transposes(srcs):
+            banks = []
+            for h in range(G // 2):
+                xt = tps.tile([P, 2, 2, P], F32, name="xt")
+                for s in range(2):
+                    view, i = srcs[2 * h + s]
+                    for u in range(2):
+                        lo = i * KW + u * P
+                        nc.tensor.transpose(xt[:, s, u, :], view[:, lo : lo + P], ident[:])
+                banks.append(xt)
+            return banks
+
+        def regroup(banks, grouped, engines):
+            for h, xt in enumerate(banks):
+                dst = grouped[:, h * 1024 : (h + 1) * 1024].bitcast(F32)
+                dst = dst.rearrange("p (s b u) -> p s b u", s=2, u=2)
+                src = xt[:].rearrange("p s u b -> p s b u")
+                if engines[h] == "v":
+                    nc.vector.tensor_copy(out=dst, in_=src)
+                else:
+                    nc.scalar.copy(out=dst, in_=src)
+
+        def quantise(grouped, codes, scales):
+            for h in range(G // 2):
+                nc.vector.quantize_mx(
+                    out=codes[:, h * 256 : (h + 1) * 256].bitcast(FP8X4),
+                    scales=scales[:, h * 256 : (h + 1) * 256],
+                    in_=grouped[:, h * 1024 : (h + 1) * 1024],
+                )
+
+        def prepare_vector(banks, codes, scales, engines):
+            grouped = stage.tile([P, G * P * 4], BF16, name="grouped", align_bytes=64)
+            regroup(banks, grouped, engines)
+            quantise(grouped, codes, scales)
+
+        w_codes = keep.tile([P, C], U32, name="w_codes", align_bytes=64)
+        w_scales = keep.tile([P, C], U8, name="w_scales", align_bytes=64)
+        ww = w_raw[:].bitcast(F32)
+        w_banks = transposes([(ww, j) for j in range(G)])
+        prepare_vector(w_banks, w_codes, w_scales, ["v", "s"])
+
+        def new_codes():
+            codes = stage.tile([P, G * P], U32, name="codes", align_bytes=64)
+            scales = stage.tile([P, G * P], U8, name="scales", align_bytes=64)
+            return codes, scales
+
+        banks = transposes(x_of_tile[0:G])
+        cur = new_codes()
+        prepare_vector(banks, cur[0], cur[1], ["v", "s"])
+
+        for g in range(NG):
+            if g + 1 < NG:
+                banks = transposes(x_of_tile[(g + 1) * G : (g + 2) * G])
+            codes, scales = cur
+            for i in range(G):
+                acc = ops.tile([P, C], F32, name="acc")
+                nc.tensor.matmul_mx(
+                    out=acc[:],
+                    lhsT=codes[:, i * P : (i + 1) * P].bitcast(FP8X4),
+                    lhsT_scale=scales[:, i * P : (i + 1) * P],
+                    rhs=w_codes[:].bitcast(FP8X4),
+                    rhs_scale=w_scales[:],
+                    start=True,
+                    stop=True,
+                )
+                c, j, last = o_of_tile[g * G + i]
+                nc.scalar.copy(out=o_tiles[c][:, j * C : (j + 1) * C], in_=acc[:])
+                if last:
+                    n = STORE_TILES[c]
+                    hi = (g * G + i + 1) * C
+                    nc.sync.dma_start(out=out_v[:, hi - n * C : hi], in_=o_tiles[c][:])
+            if g + 1 < NG:
+                cur = new_codes()
+                prepare_vector(banks, cur[0], cur[1], ["v", "v"])

@@ -17,8 +17,8 @@ KW = K // 2
 T = B // P
 G = 4
 NG = T // G
-LOAD_TILES = [4, 4, 8, 16, 32]
-STORE_TILES = [8, 8, 8, 8, 8, 8, 8, 8]
+LOAD_TILES = [8, 8, 16, 32]
+STORE_TILES = [16, 16, 16, 8, 8]
 
 FLOPS = 2 * B * C * K
 
@@ -27,7 +27,7 @@ def tile_tensoroutputlayer_t_kernel(tc, core, weights, out):
     nc = tc.nc
     core_v = core.rearrange("(p t) i j k -> p (t i j k)", t=T)
     out_v = out.rearrange("(p t) c -> p (t c)", t=T)
-    w_v = weights.rearrange("(j p) a b c -> p j (a b c)", p=P)
+    w_v = weights.rearrange("(p j) a b c -> p (j a b c)", j=G)
 
     with ExitStack() as ctx:
         keep = ctx.enter_context(tc.tile_pool(name="keep", bufs=1))
@@ -37,7 +37,7 @@ def tile_tensoroutputlayer_t_kernel(tc, core, weights, out):
         ctx.enter_context(tc.manual_schedule())
 
         w_raw = keep.tile([P, G * K], BF16, name="w_raw")
-        nc.sync.dma_start(out=w_raw[:].rearrange("p (j k) -> p j k", j=G), in_=w_v)
+        nc.sync.dma_start(out=w_raw[:], in_=w_v)
         x_of_tile = []
         t0 = 0
         for c, n in enumerate(LOAD_TILES):
@@ -98,7 +98,11 @@ def tile_tensoroutputlayer_t_kernel(tc, core, weights, out):
         w_scales = keep.tile([P, C], U8, name="w_scales", align_bytes=64)
         ww = w_raw[:].bitcast(F32)
         w_banks = transposes([(ww, j) for j in range(G)])
-        prepare_vector(w_banks, w_codes, w_scales, ["v", "s"])
+        w_grouped = stage.tile([P, G * P * 4], BF16, name="grouped", align_bytes=64)
+        w_dst = w_grouped[:].bitcast(F32).rearrange("p (b h s u) -> p h b s u", h=2, s=2, u=2)
+        for h, xt in enumerate(w_banks):
+            nc.vector.tensor_copy(out=w_dst[:, h], in_=xt[:].rearrange("p s u b -> p b s u"))
+        quantise(w_grouped, w_codes, w_scales)
 
         def new_codes():
             codes = stage.tile([P, G * P], U32, name="codes", align_bytes=64)

@@ -17,8 +17,8 @@ KW = K // 2
 T = B // P
 G = 4
 NG = T // G
-LOAD_TILES = [8, 8, 16, 32]
-STORE_TILES = [16, 16, 16, 8, 8]
+LOAD_TILES = [4, 4, 8, 16, 32]
+STORE_TILES = [8, 8, 8, 8, 8, 8, 8, 4, 2, 2]
 
 FLOPS = 2 * B * C * K
 
@@ -27,7 +27,7 @@ def tile_tensoroutputlayer_t_kernel(tc, core, weights, out):
     nc = tc.nc
     core_v = core.rearrange("(p t) i j k -> p (t i j k)", t=T)
     out_v = out.rearrange("(p t) c -> p (t c)", t=T)
-    w_v = weights.rearrange("(p j) a b c -> p (j a b c)", j=G)
+    w_v = weights.rearrange("(j p) a b c -> p j (a b c)", p=P)
 
     with ExitStack() as ctx:
         keep = ctx.enter_context(tc.tile_pool(name="keep", bufs=1))
@@ -37,7 +37,7 @@ def tile_tensoroutputlayer_t_kernel(tc, core, weights, out):
         ctx.enter_context(tc.manual_schedule())
 
         w_raw = keep.tile([P, G * K], BF16, name="w_raw")
-        nc.sync.dma_start(out=w_raw[:], in_=w_v)
+        nc.sync.dma_start(out=w_raw[:].rearrange("p (j k) -> p j k", j=G), in_=w_v)
         x_of_tile = []
         t0 = 0
         for c, n in enumerate(LOAD_TILES):
@@ -98,11 +98,7 @@ def tile_tensoroutputlayer_t_kernel(tc, core, weights, out):
         w_scales = keep.tile([P, C], U8, name="w_scales", align_bytes=64)
         ww = w_raw[:].bitcast(F32)
         w_banks = transposes([(ww, j) for j in range(G)])
-        w_grouped = stage.tile([P, G * P * 4], BF16, name="grouped", align_bytes=64)
-        w_dst = w_grouped[:].bitcast(F32).rearrange("p (b h s u) -> p h b s u", h=2, s=2, u=2)
-        for h, xt in enumerate(w_banks):
-            nc.vector.tensor_copy(out=w_dst[:, h], in_=xt[:].rearrange("p s u b -> p b s u"))
-        quantise(w_grouped, w_codes, w_scales)
+        prepare_vector(w_banks, w_codes, w_scales, ["v", "s"])
 
         def new_codes():
             codes = stage.tile([P, G * P], U32, name="codes", align_bytes=64)

@@ -17,8 +17,8 @@ KW = K // 2
 T = B // P
 G = 4
 NG = T // G
-LOAD_TILES = [4, 4, 8, 16, 32]
-STORE_TILES = [8, 8, 8, 8, 8, 8, 8, 4, 2, 2]
+LOAD_TILES = [4, 4, 8, 16, 16, 16]
+STORE_TILES = [8, 8, 8, 8, 8, 8, 8, 8]
 
 FLOPS = 2 * B * C * K
 
@@ -129,7 +129,7 @@ def tile_tensoroutputlayer_t_kernel(tc, core, weights, out):
                 if last:
                     n = STORE_TILES[c]
                     hi = (g * G + i + 1) * C
-                    nc.sync.dma_start(out=out_v[:, hi - n * C : hi], in_=o_tiles[c][:])
+                    nc.scalar.dma_start(out=out_v[:, hi - n * C : hi], in_=o_tiles[c][:])
             if g + 1 < NG:
                 cur = new_codes()
                 prepare_vector(banks, cur[0], cur[1], ["v", "v"])

from contextlib import ExitStack

import concourse.mybir as mybir
from concourse.masks import make_identity

F32 = mybir.dt.float32
BF16 = mybir.dt.bfloat16
U32 = mybir.dt.uint32
U8 = mybir.dt.uint8
FP8X4 = mybir.dt.float8_e4m3fn_x4

P = 128
B = 8192
C = 512
K = 512
KW = K // 2
T = B // P
G = 4
NG = T // G
LOAD_TILES = [4, 4, 8, 16, 16, 16]
STORE_TILES = [8, 8, 8, 8, 8, 8, 8, 8]

FLOPS = 2 * B * C * K


def tile_tensoroutputlayer_t_kernel(tc, core, weights, out):
    nc = tc.nc
    core_v = core.rearrange("(p t) i j k -> p (t i j k)", t=T)
    out_v = out.rearrange("(p t) c -> p (t c)", t=T)
    w_v = weights.rearrange("(j p) a b c -> p j (a b c)", p=P)

    with ExitStack() as ctx:
        keep = ctx.enter_context(tc.tile_pool(name="keep", bufs=1))
        stage = ctx.enter_context(tc.tile_pool(name="stage", bufs=3))
        tps = ctx.enter_context(tc.psum_pool(name="tps", bufs=4))
        ops = ctx.enter_context(tc.psum_pool(name="ops", bufs=4))
        ctx.enter_context(tc.manual_schedule())

        w_raw = keep.tile([P, G * K], BF16, name="w_raw")
        nc.sync.dma_start(out=w_raw[:].rearrange("p (j k) -> p j k", j=G), in_=w_v)
        x_of_tile = []
        t0 = 0
        for c, n in enumerate(LOAD_TILES):
            x = keep.tile([P, n * K], BF16, name="x%d" % c)
            nc.sync.dma_start(out=x[:], in_=core_v[:, t0 * K : (t0 + n) * K])
            xw = x[:].bitcast(F32)
            for i in range(n):
                x_of_tile.append((xw, i))
            t0 += n

        ident = keep.tile([P, P], F32, name="ident")
        make_identity(nc, ident[:])

        o_of_tile = []
        o_tiles = []
        for c, n in enumerate(STORE_TILES):
            o = keep.tile([P, n * C], F32, name="o%d" % c)
            o_tiles.append(o)
            for i in range(n):
                o_of_tile.append((c, i, i == n - 1))

        def transposes(srcs):
            banks = []
            for h in range(G // 2):
                xt = tps.tile([P, 2, 2, P], F32, name="xt")
                for s in range(2):
                    view, i = srcs[2 * h + s]
                    for u in range(2):
                        lo = i * KW + u * P
                        nc.tensor.transpose(xt[:, s, u, :], view[:, lo : lo + P], ident[:])
                banks.append(xt)
            return banks

        def regroup(banks, grouped, engines):
            for h, xt in enumerate(banks):
                dst = grouped[:, h * 1024 : (h + 1) * 1024].bitcast(F32)
                dst = dst.rearrange("p (s b u) -> p s b u", s=2, u=2)
                src = xt[:].rearrange("p s u b -> p s b u")
                if engines[h] == "v":
                    nc.vector.tensor_copy(out=dst, in_=src)
                else:
                    nc.scalar.copy(out=dst, in_=src)

        def quantise(grouped, codes, scales):
            for h in range(G // 2):
                nc.vector.quantize_mx(
                    out=codes[:, h * 256 : (h + 1) * 256].bitcast(FP8X4),
                    scales=scales[:, h * 256 : (h + 1) * 256],
                    in_=grouped[:, h * 1024 : (h + 1) * 1024],
                )

        def prepare_vector(banks, codes, scales, engines):
            grouped = stage.tile([P, G * P * 4], BF16, name="grouped", align_bytes=64)
            regroup(banks, grouped, engines)
            quantise(grouped, codes, scales)

        w_codes = keep.tile([P, C], U32, name="w_codes", align_bytes=64)
        w_scales = keep.tile([P, C], U8, name="w_scales", align_bytes=64)
        ww = w_raw[:].bitcast(F32)
        w_banks = transposes([(ww, j) for j in range(G)])
        prepare_vector(w_banks, w_codes, w_scales, ["v", "s"])

        def new_codes():
            codes = stage.tile([P, G * P], U32, name="codes", align_bytes=64)
            scales = stage.tile([P, G * P], U8, name="scales", align_bytes=64)
            return codes, scales

        banks = transposes(x_of_tile[0:G])
        cur = new_codes()
        prepare_vector(banks, cur[0], cur[1], ["v", "s"])

        for g in range(NG):
            if g + 1 < NG:
                banks = transposes(x_of_tile[(g + 1) * G : (g + 2) * G])
            codes, scales = cur
            for i in range(G):
                acc = ops.tile([P, C], F32, name="acc")
                nc.tensor.matmul_mx(
                    out=acc[:],
                    lhsT=codes[:, i * P : (i + 1) * P].bitcast(FP8X4),
                    lhsT_scale=scales[:, i * P : (i + 1) * P],
                    rhs=w_codes[:].bitcast(FP8X4),
                    rhs_scale=w_scales[:],
                    start=True,
                    stop=True,
                )
                c, j, last = o_of_tile[g * G + i]
                nc.scalar.copy(out=o_tiles[c][:, j * C : (j + 1) * C], in_=acc[:])
                if last:
                    n = STORE_TILES[c]
                    hi = (g * G + i + 1) * C
                    nc.scalar.dma_start(out=out_v[:, hi - n * C : hi], in_=o_tiles[c][:])
            if g + 1 < NG:
                cur = new_codes()
                prepare_vector(banks, cur[0], cur[1], ["v", "v"])
